import numpy as np
import ml_dtypes


def mxq(x, axis, fmt="e4m3"):
    dtype, down = {"e4m3": (ml_dtypes.float8_e4m3fn, 7), "e5m2": (ml_dtypes.float8_e5m2, 14)}[fmt]
    v = np.moveaxis(np.asarray(x, np.float32).astype(ml_dtypes.bfloat16).astype(np.float64), axis, -1)
    blocks = v.reshape(v.shape[:-1] + (-1, 32))
    amax = np.abs(blocks).max(-1, keepdims=True)
    byte = np.maximum(np.where(amax > 0, np.frexp(amax)[1] - 1 + 127, 0) - down, 1)
    scale = np.exp2(byte - 127.0)
    codes = (blocks / scale).astype(np.float32).astype(dtype).astype(np.float64)
    return np.moveaxis((codes * scale).reshape(v.shape), -1, axis)


WIDE = False


def mx_kscale(k):
    if not WIDE:
        return np.ones(k)
    levels = np.array([10, -10, 5, -5, 0])
    if k % 512:
        return np.exp2(np.random.permutation(np.resize(levels, k // 32))).repeat(32)
    a = np.empty((k // 512, 16))
    for p in range(k // 512):
        a[p, :8] = np.random.permutation(np.resize(levels, 8))
        for g in range(8):
            far = levels[np.abs(levels - a[p, g]) >= 10]
            a[p, g + 8] = far[np.random.randint(len(far))]
    return np.exp2(a.ravel()).repeat(32)


BF16 = ml_dtypes.bfloat16


def bf(x):
    return np.asarray(x, np.float32).astype(BF16)


def f64(x):
    return np.asarray(x).astype(np.float64)


B, N, T, D, DO, H, E = 128, 2, 8, 512, 512, 8, 128
S = N * T


def sigmoid(v):
    return 1.0 / (1.0 + np.exp(-v))


def setup_inputs():
    r = np.random.standard_normal
    s = mx_kscale(D)
    return {
        "x": bf(r((B, S, D)) * s),
        "edge_features": bf(r((B, E))),
        "Wv": bf(r((D, DO)) / np.sqrt(D) / s[:, None]),
        "bv": bf(r(DO) * 0.3),
        "Wgate": bf(r((E, DO)) / np.sqrt(E)),
        "bgate": bf(r(DO) * 0.3),
        "Wscale": bf(r((E, DO)) * 0.7 / np.sqrt(E)),
        "bscale": bf(r(DO) * 0.3),
        "Wshift": bf(r((E, DO)) * 0.7 / np.sqrt(E)),
        "bshift": bf(r(DO) * 0.3),
    }


def reference(x, edge_features, Wv, bv, Wgate, bgate, Wscale, bscale, Wshift, bshift):
    e = f64(edge_features)
    v = (mxq(f64(x).reshape(B * S, D), 1, "e4m3") @ mxq(f64(Wv), 0, "e4m3")).reshape(B, S, DO) + f64(bv)
    gate = sigmoid(e @ f64(Wgate) + f64(bgate))
    scale = np.tanh(e @ f64(Wscale) + f64(bscale))
    shift = e @ f64(Wshift) + f64(bshift)
    return (v * (1.0 + scale[:, None, :]) + shift[:, None, :]) * gate[:, None, :]

@@ -1,0 +1,207 @@
+from contextlib import ExitStack
+
+import concourse.mybir as mybir
+from concourse.masks import make_identity
+
+F32 = mybir.dt.float32
+BF16 = mybir.dt.bfloat16
+U32 = mybir.dt.uint32
+U8 = mybir.dt.uint8
+FP8X4 = mybir.dt.float8_e4m3fn_x4
+ACT = mybir.ActivationFunctionType
+ALU = mybir.AluOpType
+
+P = 128
+B, S, D, DO, E = 128, 16, 512, 512, 128
+PACK = 4
+HALVES = 2
+ROWS = 2
+ROUNDS = S // ROWS
+CHUNKS = DO // P
+RUN = 4
+EARLY_ROUNDS = 2
+ADD_LAG = 3
+
+FLOPS = 2 * B * S * D * DO + 3 * 2 * B * E * DO
+
+
+def tile_graphditunit_pa_kernel(
+    tc, x, edge_features, Wv, bv, Wgate, bgate, Wscale, bscale, Wshift, bshift, out
+):
+    nc = tc.nc
+    with ExitStack() as ctx:
+        ctx.enter_context(tc.manual_schedule())
+        const = ctx.enter_context(tc.tile_pool(name="const", bufs=1))
+        per_round = ctx.enter_context(tc.tile_pool(name="per_round", bufs=ROUNDS))
+        per_row = ctx.enter_context(tc.tile_pool(name="per_row", bufs=S))
+        psum_add = ctx.enter_context(tc.psum_pool(name="psum_add", bufs=1))
+        psum = ctx.enter_context(tc.psum_pool(name="psum", bufs=7))
+
+        ident_bf16 = const.tile([P, P], BF16)
+        make_identity(nc, ident_bf16[:])
+        ident_f32 = const.tile([P, P], F32)
+        make_identity(nc, ident_f32[:])
+        bv_rows = const.tile([P, P], BF16)
+        nc.vector.memset(bv_rows[:], 0.0)
+        nc.scalar.dma_start(out=bv_rows[0:CHUNKS, :], in_=bv.rearrange("(c n) -> c n", n=P))
+        bias_planes = []
+        for bias in (bgate, bscale, bshift):
+            plane = const.tile([P, DO], BF16, tag="plane", bufs=3)
+            nc.vector.memset(plane[:], 0.0)
+            nc.scalar.dma_start(out=plane[0:1, :], in_=bias.rearrange("(o c) -> o c", o=1))
+            bias_planes.append(plane)
+        ones = const.tile([P, P], BF16)
+        nc.vector.memset(ones[:], 1.0)
+        warm = const.tile([P, 1], F32)
+        nc.vector.memset(warm[:], 0.0)
+        nc.scalar.activation(out=warm[:], in_=warm[:], func=ACT.Sigmoid)
+
+        e_sb = const.tile([P, E], BF16)
+        nc.sync.dma_start(out=e_sb[:], in_=edge_features)
+        w_mod = const.tile([P, 3, DO], BF16)
+        nc.sync.dma_start(out=w_mod[:, 0, :], in_=Wgate)
+        nc.sync.dma_start(out=w_mod[:, 1, :], in_=Wscale)
+        w_raw = const.tile([P, PACK, DO], BF16)
+        nc.sync.dma_start(
+            out=w_raw[:].rearrange("p t c -> p (t c)"),
+            in_=Wv.rearrange("(p t) c -> p (t c)", t=PACK),
+        )
+        nc.sync.dma_start(out=w_mod[:, 2, :], in_=Wshift)
+        x_tiles = []
+        for r in range(ROUNDS):
+            x_r = per_round.tile([P, ROWS * D], BF16)
+            nc.sync.dma_start(
+                out=x_r[:], in_=x[:, r * ROWS : (r + 1) * ROWS, :].rearrange("b i k -> b (i k)")
+            )
+            x_tiles.append(x_r)
+
+        small_t = psum.tile([P, 2, P], BF16, tag="bank")
+        nc.tensor.transpose(small_t[:, 0, :], e_sb[:], ident_bf16[:])
+        nc.tensor.transpose(small_t[:, 1, :], bv_rows[:], ident_bf16[:])
+        e_t = const.tile([P, B], BF16)
+        nc.vector.tensor_copy(out=e_t[:], in_=small_t[:, 0, :])
+        bv_t = const.tile([P, CHUNKS], F32)
+        nc.vector.tensor_copy(out=bv_t[:], in_=small_t[:, 1, 0:CHUNKS])
+        bv_rep = const.tile([P, CHUNKS, P], F32)
+        nc.vector.tensor_copy(out=bv_rep[:], in_=bv_t[:].unsqueeze(2).to_broadcast([P, CHUNKS, P]))
+
+        def edge_matmul(j):
+            pre_j = psum.tile([P, DO], F32, tag="bank")
+            nc.tensor.matmul(out=pre_j[:], lhsT=e_t[:], rhs=w_mod[:, j, :], start=True, stop=False)
+            nc.tensor.matmul(out=pre_j[:], lhsT=ones[:], rhs=bias_planes[j][:], start=False, stop=True)
+            return pre_j
+
+        pre_gate = edge_matmul(0)
+        gate = const.tile([P, DO], F32)
+        nc.scalar.activation(out=gate[:], in_=pre_gate[:], func=ACT.Sigmoid)
+        pre_scale = edge_matmul(1)
+        scale = const.tile([P, DO], F32)
+        nc.scalar.activation(out=scale[:], in_=pre_scale[:], func=ACT.Tanh)
+
+        w_grouped = const.tile([P, DO, PACK], BF16, align_bytes=64)
+        nc.vector.tensor_copy(
+            out=w_grouped[:].rearrange("p (c i) t -> p c t i", i=RUN),
+            in_=w_raw[:].rearrange("p t (c i) -> p c t i", i=RUN),
+        )
+        w_codes = const.tile([P, DO], U32, align_bytes=64)
+        w_scales = const.tile([P, DO], U8, align_bytes=64)
+        nc.vector.quantize_mx(
+            out=w_codes[:].bitcast(FP8X4),
+            scales=w_scales[:],
+            in_=w_grouped[:].rearrange("p c t -> p (c t)"),
+        )
+
+        x_grouped = []
+
+        def transpose_x(r):
+            x_words = x_tiles[r][:].bitcast(F32)
+            x_t = psum.tile([P, ROWS, HALVES, B], F32, tag="bank")
+            for i in range(ROWS):
+                for u in range(HALVES):
+                    words = slice(i * HALVES * P + u, (i + 1) * HALVES * P, HALVES)
+                    nc.tensor.transpose(x_t[:, i, u, :], x_words[:, words], ident_f32[:])
+            grouped_r = per_round.tile([P, ROWS * B * PACK], BF16, align_bytes=64)
+            nc.scalar.copy(
+                out=grouped_r[:].bitcast(F32).rearrange("p (i b u) -> p i b u", i=ROWS, u=HALVES),
+                in_=x_t[:].rearrange("p i u b -> p i b u"),
+            )
+            x_grouped.append(grouped_r)
+
+        for r in range(EARLY_ROUNDS):
+            transpose_x(r)
+
+        shift = edge_matmul(2)
+        bv_all = psum.tile([P, CHUNKS, P], F32, tag="bank")
+        for c in range(CHUNKS):
+            nc.tensor.transpose(bv_all[:, c, :], bv_rep[:, c, :], ident_f32[:])
+        mul = const.tile([P, DO], F32)
+        nc.vector.scalar_tensor_tensor(
+            out=mul[:], in0=scale[:], scalar=1.0, in1=gate[:], op0=ALU.add, op1=ALU.mult
+        )
+        shift_gate = const.tile([P, DO], F32)
+        nc.vector.tensor_tensor(out=shift_gate[:], in0=shift[:], in1=gate[:], op=ALU.mult)
+        add = const.tile([P, DO], F32)
+        nc.vector.tensor_tensor(
+            out=add[:], in0=bv_all[:].rearrange("p c n -> p (c n)"), in1=mul[:], op=ALU.mult
+        )
+        nc.vector.tensor_tensor(out=add[:], in0=add[:], in1=shift_gate[:], op=ALU.add)
+
+        for r in range(EARLY_ROUNDS, ROUNDS):
+            transpose_x(r)
+
+        x_codes = []
+        x_scales = []
+        for r in range(ROUNDS):
+            codes_r = per_round.tile([P, ROWS * B], U32, align_bytes=64)
+            scales_r = per_round.tile([P, ROWS * B], U8, align_bytes=64)
+            nc.vector.quantize_mx(
+                out=codes_r[:].bitcast(FP8X4), scales=scales_r[:], in_=x_grouped[r][:]
+            )
+            x_codes.append(codes_r)
+            x_scales.append(scales_r)
+
+        add_t_psum = psum.tile([P, CHUNKS, B], F32, tag="bank")
+        for c in range(CHUNKS):
+            nc.tensor.transpose(add_t_psum[:, c, :], add[:, c * P : (c + 1) * P], ident_f32[:])
+        add_t = const.tile([P, CHUNKS, B], F32)
+        nc.scalar.copy(out=add_t[:], in_=add_t_psum[:])
+
+        products = []
+
+        def multiply(i):
+            r = i // ROWS
+            samples = slice((i % ROWS) * B, (i % ROWS + 1) * B)
+            acc = psum.tile([P, DO], F32, tag="bank")
+            nc.tensor.matmul_mx(
+                out=acc[:],
+                lhsT=x_codes[r][:, samples].bitcast(FP8X4),
+                lhsT_scale=x_scales[r][:, samples],
+                rhs=w_codes[:].bitcast(FP8X4),
+                rhs_scale=w_scales[:],
+                start=True,
+                stop=True,
+            )
+            o_i = per_row.tile([P, DO], F32)
+            nc.vector.tensor_tensor(out=o_i[:], in0=acc[:], in1=mul[:], op=ALU.mult)
+            products.append(o_i)
+
+        def add_and_store(i):
+            o_i = products[i]
+            if i % 2 == 0:
+                nc.gpsimd.tensor_tensor(out=o_i[:], in0=o_i[:], in1=add[:], op=ALU.add)
+            else:
+                nc.vector.tensor_tensor(
+                    out=o_i[:], in0=o_i[:], in1=add_psum[:].rearrange("p c n -> p (c n)"), op=ALU.add
+                )
+            nc.sync.dma_start(out=out[:, i, :], in_=o_i[:])
+
+        for i in range(ADD_LAG):
+            multiply(i)
+        add_psum = psum_add.tile([P, CHUNKS, P], F32)
+        for c in range(CHUNKS):
+            nc.tensor.transpose(add_psum[:, c, :], add_t[:, c, :], ident_f32[:])
+        for i in range(ADD_LAG, S):
+            multiply(i)
+            add_and_store(i - ADD_LAG)
+        for i in range(S - ADD_LAG, S):
+            add_and_store(i)

@@ -19,8 +19,6 @@ ROWS = 2
 ROUNDS = S // ROWS
 CHUNKS = DO // P
 RUN = 4
-EARLY_ROUNDS = 2
-ADD_LAG = 3
 
 FLOPS = 2 * B * S * D * DO + 3 * 2 * B * E * DO
 
@@ -34,86 +32,99 @@ def tile_graphditunit_pa_kernel(
         const = ctx.enter_context(tc.tile_pool(name="const", bufs=1))
         per_round = ctx.enter_context(tc.tile_pool(name="per_round", bufs=ROUNDS))
         per_row = ctx.enter_context(tc.tile_pool(name="per_row", bufs=S))
-        psum_add = ctx.enter_context(tc.psum_pool(name="psum_add", bufs=1))
         psum = ctx.enter_context(tc.psum_pool(name="psum", bufs=7))
+        psum_add = ctx.enter_context(tc.psum_pool(name="psum_add", bufs=1))
 
+        bias_rows = const.tile([P, P], BF16)
+        nc.vector.memset(bias_rows[:], 0.0)
+        warm = const.tile([P, 1], F32)
+        nc.vector.memset(warm[:], 0.0)
         ident_bf16 = const.tile([P, P], BF16)
         make_identity(nc, ident_bf16[:])
         ident_f32 = const.tile([P, P], F32)
         make_identity(nc, ident_f32[:])
-        bv_rows = const.tile([P, P], BF16)
-        nc.vector.memset(bv_rows[:], 0.0)
-        nc.scalar.dma_start(out=bv_rows[0:CHUNKS, :], in_=bv.rearrange("(c n) -> c n", n=P))
-        bias_planes = []
-        for bias in (bgate, bscale, bshift):
-            plane = const.tile([P, DO], BF16, tag="plane", bufs=3)
-            nc.vector.memset(plane[:], 0.0)
-            nc.scalar.dma_start(out=plane[0:1, :], in_=bias.rearrange("(o c) -> o c", o=1))
-            bias_planes.append(plane)
-        ones = const.tile([P, P], BF16)
-        nc.vector.memset(ones[:], 1.0)
-        warm = const.tile([P, 1], F32)
-        nc.vector.memset(warm[:], 0.0)
-        nc.scalar.activation(out=warm[:], in_=warm[:], func=ACT.Sigmoid)
+
+        def load_bias(j, bias):
+            nc.sync.dma_start(
+                out=bias_rows[j * CHUNKS : (j + 1) * CHUNKS, :], in_=bias.rearrange("(c n) -> c n", n=P)
+            )
 
         e_sb = const.tile([P, E], BF16)
-        nc.sync.dma_start(out=e_sb[:], in_=edge_features)
         w_mod = const.tile([P, 3, DO], BF16)
-        nc.sync.dma_start(out=w_mod[:, 0, :], in_=Wgate)
-        nc.sync.dma_start(out=w_mod[:, 1, :], in_=Wscale)
         w_raw = const.tile([P, PACK, DO], BF16)
-        nc.sync.dma_start(
-            out=w_raw[:].rearrange("p t c -> p (t c)"),
-            in_=Wv.rearrange("(p t) c -> p (t c)", t=PACK),
-        )
-        nc.sync.dma_start(out=w_mod[:, 2, :], in_=Wshift)
         x_tiles = []
-        for r in range(ROUNDS):
+
+        def load_x(r):
             x_r = per_round.tile([P, ROWS * D], BF16)
             nc.sync.dma_start(
                 out=x_r[:], in_=x[:, r * ROWS : (r + 1) * ROWS, :].rearrange("b i k -> b (i k)")
             )
             x_tiles.append(x_r)
 
-        small_t = psum.tile([P, 2, P], BF16, tag="bank")
-        nc.tensor.transpose(small_t[:, 0, :], e_sb[:], ident_bf16[:])
-        nc.tensor.transpose(small_t[:, 1, :], bv_rows[:], ident_bf16[:])
+        def load_w():
+            nc.sync.dma_start(
+                out=w_raw[:].rearrange("p t c -> p (t c)"),
+                in_=Wv.rearrange("(p t) c -> p (t c)", t=PACK),
+            )
+
+        nc.sync.dma_start(out=e_sb[:], in_=edge_features)
+        nc.sync.dma_start(out=w_mod[:, 0, :], in_=Wgate)
+        for j, bias in enumerate((bgate, bscale, bshift, bv)):
+            load_bias(j, bias)
+        load_w()
+        nc.sync.dma_start(out=w_mod[:, 1, :], in_=Wscale)
+        load_x(0)
+        nc.sync.dma_start(out=w_mod[:, 2, :], in_=Wshift)
+        for r in range(1, ROUNDS):
+            load_x(r)
+
+        nc.scalar.activation(out=warm[:], in_=warm[:], func=ACT.Sigmoid)
+
+        e_t_psum = psum.tile([P, P], BF16, tag="bank")
+        nc.tensor.transpose(e_t_psum[:], e_sb[:], ident_bf16[:])
         e_t = const.tile([P, B], BF16)
-        nc.vector.tensor_copy(out=e_t[:], in_=small_t[:, 0, :])
-        bv_t = const.tile([P, CHUNKS], F32)
-        nc.vector.tensor_copy(out=bv_t[:], in_=small_t[:, 1, 0:CHUNKS])
-        bv_rep = const.tile([P, CHUNKS, P], F32)
-        nc.vector.tensor_copy(out=bv_rep[:], in_=bv_t[:].unsqueeze(2).to_broadcast([P, CHUNKS, P]))
+        nc.vector.tensor_copy(out=e_t[:], in_=e_t_psum[:])
 
         def edge_matmul(j):
             pre_j = psum.tile([P, DO], F32, tag="bank")
             nc.tensor.matmul(out=pre_j[:], lhsT=e_t[:], rhs=w_mod[:, j, :], start=True, stop=False)
-            nc.tensor.matmul(out=pre_j[:], lhsT=ones[:], rhs=bias_planes[j][:], start=False, stop=True)
+            for c in range(CHUNKS):
+                row = j * CHUNKS + c
+                nc.tensor.matmul(
+                    out=pre_j[:, c * P : (c + 1) * P],
+                    lhsT=ident_bf16[:, row : row + 1].to_broadcast([P, P]),
+                    rhs=bias_rows[:],
+                    start=False,
+                    stop=(c == CHUNKS - 1),
+                )
             return pre_j
 
-        pre_gate = edge_matmul(0)
         gate = const.tile([P, DO], F32)
-        nc.scalar.activation(out=gate[:], in_=pre_gate[:], func=ACT.Sigmoid)
-        pre_scale = edge_matmul(1)
         scale = const.tile([P, DO], F32)
-        nc.scalar.activation(out=scale[:], in_=pre_scale[:], func=ACT.Tanh)
+        mul = const.tile([P, DO], F32)
+        add = const.tile([P, DO], F32)
+        shift_gate = const.tile([P, DO], F32)
 
         w_grouped = const.tile([P, DO, PACK], BF16, align_bytes=64)
-        nc.vector.tensor_copy(
-            out=w_grouped[:].rearrange("p (c i) t -> p c t i", i=RUN),
-            in_=w_raw[:].rearrange("p t (c i) -> p c t i", i=RUN),
-        )
         w_codes = const.tile([P, DO], U32, align_bytes=64)
         w_scales = const.tile([P, DO], U8, align_bytes=64)
-        nc.vector.quantize_mx(
-            out=w_codes[:].bitcast(FP8X4),
-            scales=w_scales[:],
-            in_=w_grouped[:].rearrange("p c t -> p (c t)"),
-        )
 
-        x_grouped = []
+        def regroup(copy, columns):
+            copy(
+                out=w_grouped[:, columns, :].rearrange("p (c i) t -> p c t i", i=RUN),
+                in_=w_raw[:, :, columns].rearrange("p t (c i) -> p c t i", i=RUN),
+            )
 
-        def transpose_x(r):
+        def quantise_w():
+            nc.vector.quantize_mx(
+                out=w_codes[:].bitcast(FP8X4),
+                scales=w_scales[:],
+                in_=w_grouped[:].rearrange("p c t -> p (c t)"),
+            )
+
+        x_grouped, x_codes, x_scales = {}, {}, {}
+
+        def transpose_x(r, copy=nc.scalar.copy):
             x_words = x_tiles[r][:].bitcast(F32)
             x_t = psum.tile([P, ROWS, HALVES, B], F32, tag="bank")
             for i in range(ROWS):
@@ -121,87 +132,196 @@ def tile_graphditunit_pa_kernel(
                     words = slice(i * HALVES * P + u, (i + 1) * HALVES * P, HALVES)
                     nc.tensor.transpose(x_t[:, i, u, :], x_words[:, words], ident_f32[:])
             grouped_r = per_round.tile([P, ROWS * B * PACK], BF16, align_bytes=64)
-            nc.scalar.copy(
+            copy(
                 out=grouped_r[:].bitcast(F32).rearrange("p (i b u) -> p i b u", i=ROWS, u=HALVES),
                 in_=x_t[:].rearrange("p i u b -> p i b u"),
             )
-            x_grouped.append(grouped_r)
+            x_grouped[r] = grouped_r
 
-        for r in range(EARLY_ROUNDS):
-            transpose_x(r)
-
-        shift = edge_matmul(2)
-        bv_all = psum.tile([P, CHUNKS, P], F32, tag="bank")
-        for c in range(CHUNKS):
-            nc.tensor.transpose(bv_all[:, c, :], bv_rep[:, c, :], ident_f32[:])
-        mul = const.tile([P, DO], F32)
-        nc.vector.scalar_tensor_tensor(
-            out=mul[:], in0=scale[:], scalar=1.0, in1=gate[:], op0=ALU.add, op1=ALU.mult
-        )
-        shift_gate = const.tile([P, DO], F32)
-        nc.vector.tensor_tensor(out=shift_gate[:], in0=shift[:], in1=gate[:], op=ALU.mult)
-        add = const.tile([P, DO], F32)
-        nc.vector.tensor_tensor(
-            out=add[:], in0=bv_all[:].rearrange("p c n -> p (c n)"), in1=mul[:], op=ALU.mult
-        )
-        nc.vector.tensor_tensor(out=add[:], in0=add[:], in1=shift_gate[:], op=ALU.add)
-
-        for r in range(EARLY_ROUNDS, ROUNDS):
-            transpose_x(r)
-
-        x_codes = []
-        x_scales = []
-        for r in range(ROUNDS):
+        def quantise_x(r):
             codes_r = per_round.tile([P, ROWS * B], U32, align_bytes=64)
             scales_r = per_round.tile([P, ROWS * B], U8, align_bytes=64)
             nc.vector.quantize_mx(
                 out=codes_r[:].bitcast(FP8X4), scales=scales_r[:], in_=x_grouped[r][:]
             )
-            x_codes.append(codes_r)
-            x_scales.append(scales_r)
+            x_codes[r], x_scales[r] = codes_r, scales_r
 
-        add_t_psum = psum.tile([P, CHUNKS, B], F32, tag="bank")
-        for c in range(CHUNKS):
-            nc.tensor.transpose(add_t_psum[:, c, :], add[:, c * P : (c + 1) * P], ident_f32[:])
-        add_t = const.tile([P, CHUNKS, B], F32)
-        nc.scalar.copy(out=add_t[:], in_=add_t_psum[:])
+        accs, results, turned = {}, {}, {}
 
-        products = []
-
-        def multiply(i):
-            r = i // ROWS
-            samples = slice((i % ROWS) * B, (i % ROWS + 1) * B)
+        def multiply(row):
+            r, i = row // ROWS, row % ROWS
+            rows = slice(i * B, (i + 1) * B)
             acc = psum.tile([P, DO], F32, tag="bank")
             nc.tensor.matmul_mx(
                 out=acc[:],
-                lhsT=x_codes[r][:, samples].bitcast(FP8X4),
-                lhsT_scale=x_scales[r][:, samples],
+                lhsT=x_codes[r][:, rows].bitcast(FP8X4),
+                lhsT_scale=x_scales[r][:, rows],
                 rhs=w_codes[:].bitcast(FP8X4),
                 rhs_scale=w_scales[:],
                 start=True,
                 stop=True,
             )
+            accs[row] = acc
+
+        def modulate(row):
             o_i = per_row.tile([P, DO], F32)
-            nc.vector.tensor_tensor(out=o_i[:], in0=acc[:], in1=mul[:], op=ALU.mult)
-            products.append(o_i)
+            nc.vector.tensor_tensor(out=o_i[:], in0=accs[row][:], in1=mul[:], op=ALU.mult)
+            results[row] = o_i
 
-        def add_and_store(i):
-            o_i = products[i]
-            if i % 2 == 0:
-                nc.gpsimd.tensor_tensor(out=o_i[:], in0=o_i[:], in1=add[:], op=ALU.add)
-            else:
+        def gpsimd_add(row):
+            nc.gpsimd.tensor_tensor(out=results[row][:], in0=results[row][:], in1=add[:], op=ALU.add)
+
+        def vector_add(row):
+            nc.vector.tensor_tensor(
+                out=results[row][:], in0=results[row][:], in1=add_psum[:].rearrange("p c n -> p (c n)"), op=ALU.add
+            )
+
+        def store(row, engine=nc.sync):
+            engine.dma_start(out=out[:, row, :], in_=results[row][:])
+
+        def turn(source, back):
+            for c in range(CHUNKS):
+                nc.tensor.transpose(back[:, c, :], source[:, c, :], ident_f32[:])
+
+        def multiply_turned(r):
+            accs[r, "t"] = []
+            for h in range(2):
+                acc = psum.tile([P, 2, ROWS * B], F32, tag="bank")
+                for j in range(2):
+                    columns = slice((2 * h + j) * P, (2 * h + j + 1) * P)
+                    nc.tensor.matmul_mx(
+                        out=acc[:, j, :],
+                        lhsT=w_codes[:, columns].bitcast(FP8X4),
+                        lhsT_scale=w_scales[:, columns],
+                        rhs=x_codes[r][:].bitcast(FP8X4),
+                        rhs_scale=x_scales[r][:],
+                        start=True,
+                        stop=True,
+                    )
+                accs[r, "t"].append(acc)
+
+        def modulate_turned(r):
+            z = per_round.tile([P, CHUNKS, ROWS, B], F32)
+            for h in range(2):
                 nc.vector.tensor_tensor(
-                    out=o_i[:], in0=o_i[:], in1=add_psum[:].rearrange("p c n -> p (c n)"), op=ALU.add
+                    out=z[:, 2 * h : 2 * h + 2, :, :],
+                    in0=accs[r, "t"][h][:].rearrange("p c (i b) -> p c i b", i=ROWS),
+                    in1=mul_t[:, 2 * h : 2 * h + 2, :].unsqueeze(2).to_broadcast([P, 2, ROWS, B]),
+                    op=ALU.mult,
                 )
-            nc.sync.dma_start(out=out[:, i, :], in_=o_i[:])
+            turned[r] = z
 
-        for i in range(ADD_LAG):
-            multiply(i)
-        add_psum = psum_add.tile([P, CHUNKS, P], F32)
+        def finish_turned(r):
+            for i in range(ROWS):
+                o_ps = psum.tile([P, CHUNKS, P], F32, tag="bank")
+                for c in range(CHUNKS):
+                    nc.tensor.matmul(
+                        out=o_ps[:, c, :], lhsT=add_t[:, c, :], rhs=ident_f32[:],
+                        start=True, stop=False, is_transpose=True,
+                    )
+                    nc.tensor.matmul(
+                        out=o_ps[:, c, :], lhsT=turned[r][:, c, i, :], rhs=ident_f32[:],
+                        start=False, stop=True, is_transpose=True,
+                    )
+                o_i = per_row.tile([P, DO], F32)
+                nc.scalar.copy(out=o_i[:], in_=o_ps[:].rearrange("p c n -> p (c n)"))
+                results[r * ROWS + i] = o_i
+                store(r * ROWS + i, nc.scalar)
+
+        pre_gate = edge_matmul(0)
+        nc.scalar.activation(out=gate[:], in_=pre_gate[:], func=ACT.Sigmoid)
+        pre_scale = edge_matmul(1)
+        nc.scalar.activation(out=scale[:], in_=pre_scale[:], func=ACT.Tanh)
+        regroup(nc.vector.tensor_copy, slice(0, DO))
+        quantise_w()
+        transpose_x(0)
+        nc.vector.scalar_tensor_tensor(
+            out=mul[:], in0=scale[:], scalar=1.0, in1=gate[:], op0=ALU.add, op1=ALU.mult
+        )
+        transpose_x(1)
+        quantise_x(0)
+        shift = edge_matmul(2)
+        bv_t_psum = psum.tile([P, P], BF16, tag="bank")
+        nc.tensor.transpose(bv_t_psum[:], bias_rows[:], ident_bf16[:])
+        bv_t = const.tile([P, CHUNKS], F32)
+        nc.scalar.copy(out=bv_t[:], in_=bv_t_psum[:, 3 * CHUNKS : 4 * CHUNKS])
+        transpose_x(2)
+        quantise_x(1)
+        bv_all = psum.tile([P, CHUNKS, P], F32, tag="bank")
         for c in range(CHUNKS):
-            nc.tensor.transpose(add_psum[:, c, :], add_t[:, c, :], ident_f32[:])
-        for i in range(ADD_LAG, S):
-            multiply(i)
-            add_and_store(i - ADD_LAG)
-        for i in range(S - ADD_LAG, S):
-            add_and_store(i)
+            nc.tensor.transpose(bv_all[:, c, :], bv_t[:, c : c + 1].to_broadcast([P, P]), ident_f32[:])
+        transpose_x(3)
+        nc.vector.tensor_tensor(out=shift_gate[:], in0=shift[:], in1=gate[:], op=ALU.mult)
+        quantise_x(2)
+        transpose_x(4)
+        nc.vector.tensor_tensor(
+            out=add[:], in0=bv_all[:].rearrange("p c n -> p (c n)"), in1=mul[:], op=ALU.mult
+        )
+        quantise_x(3)
+        multiply(0)
+        multiply(1)
+        transpose_x(5)
+        nc.vector.tensor_tensor(out=add[:], in0=add[:], in1=shift_gate[:], op=ALU.add)
+        quantise_x(4)
+        transpose_x(6)
+        quantise_x(5)
+        transpose_x(7)
+        mul_t_psum = psum.tile([P, CHUNKS, B], F32, tag="bank")
+        turn(mul[:].rearrange("p (c n) -> p c n", n=P), mul_t_psum)
+        mul_t = const.tile([P, CHUNKS, B], F32)
+        nc.scalar.copy(out=mul_t[:], in_=mul_t_psum[:])
+        multiply_turned(1)
+        quantise_x(6)
+        quantise_x(7)
+        add_t_psum = psum.tile([P, CHUNKS, B], F32, tag="bank")
+        turn(add[:].rearrange("p (c n) -> p c n", n=P), add_t_psum)
+        add_t = const.tile([P, CHUNKS, B], F32)
+        nc.scalar.copy(out=add_t[:], in_=add_t_psum[:])
+        modulate(0)
+        modulate(1)
+        gpsimd_add(0)
+        store(0)
+        gpsimd_add(1)
+        store(1)
+        multiply(4)
+        multiply(5)
+        modulate_turned(1)
+        multiply_turned(3)
+        modulate(4)
+        modulate(5)
+        gpsimd_add(4)
+        store(4)
+        gpsimd_add(5)
+        store(5)
+        finish_turned(1)
+        multiply(8)
+        multiply(9)
+        modulate_turned(3)
+        multiply_turned(5)
+        modulate(8)
+        modulate(9)
+        gpsimd_add(8)
+        store(8)
+        gpsimd_add(9)
+        store(9)
+        finish_turned(3)
+        multiply(12)
+        multiply(13)
+        modulate_turned(5)
+        multiply(14)
+        multiply(15)
+        add_psum = psum_add.tile([P, CHUNKS, P], F32)
+        turn(add_t, add_psum)
+        modulate(12)
+        modulate(13)
+        gpsimd_add(12)
+        store(12)
+        gpsimd_add(13)
+        store(13)
+        finish_turned(5)
+        modulate(14)
+        modulate(15)
+        vector_add(14)
+        store(14, nc.scalar)
+        vector_add(15)
+        store(15, nc.scalar)

@@ -258,8 +258,6 @@ def tile_graphditunit_pa_kernel(
             out=add[:], in0=bv_all[:].rearrange("p c n -> p (c n)"), in1=mul[:], op=ALU.mult
         )
         quantise_x(3)
-        multiply(0)
-        multiply(1)
         transpose_x(5)
         nc.vector.tensor_tensor(out=add[:], in0=add[:], in1=shift_gate[:], op=ALU.add)
         quantise_x(4)
@@ -270,6 +268,8 @@ def tile_graphditunit_pa_kernel(
         turn(mul[:].rearrange("p (c n) -> p c n", n=P), mul_t_psum)
         mul_t = const.tile([P, CHUNKS, B], F32)
         nc.scalar.copy(out=mul_t[:], in_=mul_t_psum[:])
+        multiply(0)
+        multiply(1)
         multiply_turned(1)
         quantise_x(6)
         quantise_x(7)
@@ -316,9 +316,9 @@ def tile_graphditunit_pa_kernel(
         modulate(13)
         gpsimd_add(12)
         store(12)
-        gpsimd_add(13)
-        store(13)
         finish_turned(5)
+        vector_add(13)
+        store(13, nc.scalar)
         modulate(14)
         modulate(15)
         vector_add(14)

from contextlib import ExitStack

import concourse.mybir as mybir
from concourse.masks import make_identity

F32 = mybir.dt.float32
BF16 = mybir.dt.bfloat16
U32 = mybir.dt.uint32
U8 = mybir.dt.uint8
FP8X4 = mybir.dt.float8_e4m3fn_x4
ACT = mybir.ActivationFunctionType
ALU = mybir.AluOpType

P = 128
B, S, D, DO, E = 128, 16, 512, 512, 128
PACK = 4
HALVES = 2
ROWS = 2
ROUNDS = S // ROWS
CHUNKS = DO // P
RUN = 4

FLOPS = 2 * B * S * D * DO + 3 * 2 * B * E * DO


def tile_graphditunit_pa_kernel(
    tc, x, edge_features, Wv, bv, Wgate, bgate, Wscale, bscale, Wshift, bshift, out
):
    nc = tc.nc
    with ExitStack() as ctx:
        ctx.enter_context(tc.manual_schedule())
        const = ctx.enter_context(tc.tile_pool(name="const", bufs=1))
        per_round = ctx.enter_context(tc.tile_pool(name="per_round", bufs=ROUNDS))
        per_row = ctx.enter_context(tc.tile_pool(name="per_row", bufs=S))
        psum = ctx.enter_context(tc.psum_pool(name="psum", bufs=7))
        psum_add = ctx.enter_context(tc.psum_pool(name="psum_add", bufs=1))

        bias_rows = const.tile([P, P], BF16)
        nc.vector.memset(bias_rows[:], 0.0)
        warm = const.tile([P, 1], F32)
        nc.vector.memset(warm[:], 0.0)
        ident_bf16 = const.tile([P, P], BF16)
        make_identity(nc, ident_bf16[:])
        ident_f32 = const.tile([P, P], F32)
        make_identity(nc, ident_f32[:])

        def load_bias(j, bias):
            nc.sync.dma_start(
                out=bias_rows[j * CHUNKS : (j + 1) * CHUNKS, :], in_=bias.rearrange("(c n) -> c n", n=P)
            )

        e_sb = const.tile([P, E], BF16)
        w_mod = const.tile([P, 3, DO], BF16)
        w_raw = const.tile([P, PACK, DO], BF16)
        x_tiles = []

        def load_x(r):
            x_r = per_round.tile([P, ROWS * D], BF16)
            nc.sync.dma_start(
                out=x_r[:], in_=x[:, r * ROWS : (r + 1) * ROWS, :].rearrange("b i k -> b (i k)")
            )
            x_tiles.append(x_r)

        def load_w():
            nc.sync.dma_start(
                out=w_raw[:].rearrange("p t c -> p (t c)"),
                in_=Wv.rearrange("(p t) c -> p (t c)", t=PACK),
            )

        nc.sync.dma_start(out=e_sb[:], in_=edge_features)
        nc.sync.dma_start(out=w_mod[:, 0, :], in_=Wgate)
        for j, bias in enumerate((bgate, bscale, bshift, bv)):
            load_bias(j, bias)
        load_w()
        nc.sync.dma_start(out=w_mod[:, 1, :], in_=Wscale)
        load_x(0)
        nc.sync.dma_start(out=w_mod[:, 2, :], in_=Wshift)
        for r in range(1, ROUNDS):
            load_x(r)

        nc.scalar.activation(out=warm[:], in_=warm[:], func=ACT.Sigmoid)

        e_t_psum = psum.tile([P, P], BF16, tag="bank")
        nc.tensor.transpose(e_t_psum[:], e_sb[:], ident_bf16[:])
        e_t = const.tile([P, B], BF16)
        nc.vector.tensor_copy(out=e_t[:], in_=e_t_psum[:])

        def edge_matmul(j):
            pre_j = psum.tile([P, DO], F32, tag="bank")
            nc.tensor.matmul(out=pre_j[:], lhsT=e_t[:], rhs=w_mod[:, j, :], start=True, stop=False)
            for c in range(CHUNKS):
                row = j * CHUNKS + c
                nc.tensor.matmul(
                    out=pre_j[:, c * P : (c + 1) * P],
                    lhsT=ident_bf16[:, row : row + 1].to_broadcast([P, P]),
                    rhs=bias_rows[:],
                    start=False,
                    stop=(c == CHUNKS - 1),
                )
            return pre_j

        gate = const.tile([P, DO], F32)
        scale = const.tile([P, DO], F32)
        mul = const.tile([P, DO], F32)
        add = const.tile([P, DO], F32)
        shift_gate = const.tile([P, DO], F32)

        w_grouped = const.tile([P, DO, PACK], BF16, align_bytes=64)
        w_codes = const.tile([P, DO], U32, align_bytes=64)
        w_scales = const.tile([P, DO], U8, align_bytes=64)

        def regroup(copy, columns):
            copy(
                out=w_grouped[:, columns, :].rearrange("p (c i) t -> p c t i", i=RUN),
                in_=w_raw[:, :, columns].rearrange("p t (c i) -> p c t i", i=RUN),
            )

        def quantise_w():
            nc.vector.quantize_mx(
                out=w_codes[:].bitcast(FP8X4),
                scales=w_scales[:],
                in_=w_grouped[:].rearrange("p c t -> p (c t)"),
            )

        x_grouped, x_codes, x_scales = {}, {}, {}

        def transpose_x(r, copy=nc.scalar.copy):
            x_words = x_tiles[r][:].bitcast(F32)
            x_t = psum.tile([P, ROWS, HALVES, B], F32, tag="bank")
            for i in range(ROWS):
                for u in range(HALVES):
                    words = slice(i * HALVES * P + u, (i + 1) * HALVES * P, HALVES)
                    nc.tensor.transpose(x_t[:, i, u, :], x_words[:, words], ident_f32[:])
            grouped_r = per_round.tile([P, ROWS * B * PACK], BF16, align_bytes=64)
            copy(
                out=grouped_r[:].bitcast(F32).rearrange("p (i b u) -> p i b u", i=ROWS, u=HALVES),
                in_=x_t[:].rearrange("p i u b -> p i b u"),
            )
            x_grouped[r] = grouped_r

        def quantise_x(r):
            codes_r = per_round.tile([P, ROWS * B], U32, align_bytes=64)
            scales_r = per_round.tile([P, ROWS * B], U8, align_bytes=64)
            nc.vector.quantize_mx(
                out=codes_r[:].bitcast(FP8X4), scales=scales_r[:], in_=x_grouped[r][:]
            )
            x_codes[r], x_scales[r] = codes_r, scales_r

        accs, results, turned = {}, {}, {}

        def multiply(row):
            r, i = row // ROWS, row % ROWS
            rows = slice(i * B, (i + 1) * B)
            acc = psum.tile([P, DO], F32, tag="bank")
            nc.tensor.matmul_mx(
                out=acc[:],
                lhsT=x_codes[r][:, rows].bitcast(FP8X4),
                lhsT_scale=x_scales[r][:, rows],
                rhs=w_codes[:].bitcast(FP8X4),
                rhs_scale=w_scales[:],
                start=True,
                stop=True,
            )
            accs[row] = acc

        def modulate(row):
            o_i = per_row.tile([P, DO], F32)
            nc.vector.tensor_tensor(out=o_i[:], in0=accs[row][:], in1=mul[:], op=ALU.mult)
            results[row] = o_i

        def gpsimd_add(row):
            nc.gpsimd.tensor_tensor(out=results[row][:], in0=results[row][:], in1=add[:], op=ALU.add)

        def vector_add(row):
            nc.vector.tensor_tensor(
                out=results[row][:], in0=results[row][:], in1=add_psum[:].rearrange("p c n -> p (c n)"), op=ALU.add
            )

        def store(row, engine=nc.sync):
            engine.dma_start(out=out[:, row, :], in_=results[row][:])

        def turn(source, back):
            for c in range(CHUNKS):
                nc.tensor.transpose(back[:, c, :], source[:, c, :], ident_f32[:])

        def multiply_turned(r):
            accs[r, "t"] = []
            for h in range(2):
                acc = psum.tile([P, 2, ROWS * B], F32, tag="bank")
                for j in range(2):
                    columns = slice((2 * h + j) * P, (2 * h + j + 1) * P)
                    nc.tensor.matmul_mx(
                        out=acc[:, j, :],
                        lhsT=w_codes[:, columns].bitcast(FP8X4),
                        lhsT_scale=w_scales[:, columns],
                        rhs=x_codes[r][:].bitcast(FP8X4),
                        rhs_scale=x_scales[r][:],
                        start=True,
                        stop=True,
                    )
                accs[r, "t"].append(acc)

        def modulate_turned(r):
            z = per_round.tile([P, CHUNKS, ROWS, B], F32)
            for h in range(2):
                nc.vector.tensor_tensor(
                    out=z[:, 2 * h : 2 * h + 2, :, :],
                    in0=accs[r, "t"][h][:].rearrange("p c (i b) -> p c i b", i=ROWS),
                    in1=mul_t[:, 2 * h : 2 * h + 2, :].unsqueeze(2).to_broadcast([P, 2, ROWS, B]),
                    op=ALU.mult,
                )
            turned[r] = z

        def finish_turned(r):
            for i in range(ROWS):
                o_ps = psum.tile([P, CHUNKS, P], F32, tag="bank")
                for c in range(CHUNKS):
                    nc.tensor.matmul(
                        out=o_ps[:, c, :], lhsT=add_t[:, c, :], rhs=ident_f32[:],
                        start=True, stop=False, is_transpose=True,
                    )
                    nc.tensor.matmul(
                        out=o_ps[:, c, :], lhsT=turned[r][:, c, i, :], rhs=ident_f32[:],
                        start=False, stop=True, is_transpose=True,
                    )
                o_i = per_row.tile([P, DO], F32)
                nc.scalar.copy(out=o_i[:], in_=o_ps[:].rearrange("p c n -> p (c n)"))
                results[r * ROWS + i] = o_i
                store(r * ROWS + i, nc.scalar)

        pre_gate = edge_matmul(0)
        nc.scalar.activation(out=gate[:], in_=pre_gate[:], func=ACT.Sigmoid)
        pre_scale = edge_matmul(1)
        nc.scalar.activation(out=scale[:], in_=pre_scale[:], func=ACT.Tanh)
        regroup(nc.vector.tensor_copy, slice(0, DO))
        quantise_w()
        transpose_x(0)
        nc.vector.scalar_tensor_tensor(
            out=mul[:], in0=scale[:], scalar=1.0, in1=gate[:], op0=ALU.add, op1=ALU.mult
        )
        transpose_x(1)
        quantise_x(0)
        shift = edge_matmul(2)
        bv_t_psum = psum.tile([P, P], BF16, tag="bank")
        nc.tensor.transpose(bv_t_psum[:], bias_rows[:], ident_bf16[:])
        bv_t = const.tile([P, CHUNKS], F32)
        nc.scalar.copy(out=bv_t[:], in_=bv_t_psum[:, 3 * CHUNKS : 4 * CHUNKS])
        transpose_x(2)
        quantise_x(1)
        bv_all = psum.tile([P, CHUNKS, P], F32, tag="bank")
        for c in range(CHUNKS):
            nc.tensor.transpose(bv_all[:, c, :], bv_t[:, c : c + 1].to_broadcast([P, P]), ident_f32[:])
        transpose_x(3)
        nc.vector.tensor_tensor(out=shift_gate[:], in0=shift[:], in1=gate[:], op=ALU.mult)
        quantise_x(2)
        transpose_x(4)
        nc.vector.tensor_tensor(
            out=add[:], in0=bv_all[:].rearrange("p c n -> p (c n)"), in1=mul[:], op=ALU.mult
        )
        quantise_x(3)
        transpose_x(5)
        nc.vector.tensor_tensor(out=add[:], in0=add[:], in1=shift_gate[:], op=ALU.add)
        quantise_x(4)
        transpose_x(6)
        quantise_x(5)
        transpose_x(7)
        mul_t_psum = psum.tile([P, CHUNKS, B], F32, tag="bank")
        turn(mul[:].rearrange("p (c n) -> p c n", n=P), mul_t_psum)
        mul_t = const.tile([P, CHUNKS, B], F32)
        nc.scalar.copy(out=mul_t[:], in_=mul_t_psum[:])
        multiply(0)
        multiply(1)
        multiply_turned(1)
        quantise_x(6)
        quantise_x(7)
        add_t_psum = psum.tile([P, CHUNKS, B], F32, tag="bank")
        turn(add[:].rearrange("p (c n) -> p c n", n=P), add_t_psum)
        add_t = const.tile([P, CHUNKS, B], F32)
        nc.scalar.copy(out=add_t[:], in_=add_t_psum[:])
        modulate(0)
        modulate(1)
        gpsimd_add(0)
        store(0)
        gpsimd_add(1)
        store(1)
        multiply(4)
        multiply(5)
        modulate_turned(1)
        multiply_turned(3)
        modulate(4)
        modulate(5)
        gpsimd_add(4)
        store(4)
        gpsimd_add(5)
        store(5)
        finish_turned(1)
        multiply(8)
        multiply(9)
        modulate_turned(3)
        multiply_turned(5)
        modulate(8)
        modulate(9)
        gpsimd_add(8)
        store(8)
        gpsimd_add(9)
        store(9)
        finish_turned(3)
        multiply(12)
        multiply(13)
        modulate_turned(5)
        multiply(14)
        multiply(15)
        add_psum = psum_add.tile([P, CHUNKS, P], F32)
        turn(add_t, add_psum)
        modulate(12)
        modulate(13)
        gpsimd_add(12)
        store(12)
        finish_turned(5)
        vector_add(13)
        store(13, nc.scalar)
        modulate(14)
        modulate(15)
        vector_add(14)
        store(14, nc.scalar)
        vector_add(15)
        store(15, nc.scalar)
